import numpy as np
import ml_dtypes


def mxq(x, axis, fmt="e4m3"):
    dtype, down = {"e4m3": (ml_dtypes.float8_e4m3fn, 7), "e5m2": (ml_dtypes.float8_e5m2, 14)}[fmt]
    v = np.moveaxis(np.asarray(x, np.float32).astype(ml_dtypes.bfloat16).astype(np.float64), axis, -1)
    blocks = v.reshape(v.shape[:-1] + (-1, 32))
    amax = np.abs(blocks).max(-1, keepdims=True)
    byte = np.maximum(np.where(amax > 0, np.frexp(amax)[1] - 1 + 127, 0) - down, 1)
    scale = np.exp2(byte - 127.0)
    codes = (blocks / scale).astype(np.float32).astype(dtype).astype(np.float64)
    return np.moveaxis((codes * scale).reshape(v.shape), -1, axis)


WIDE = False


def mx_kscale(k):
    if not WIDE:
        return np.ones(k)
    levels = np.array([10, -10, 5, -5, 0])
    a = np.random.permutation(np.resize(levels, k // 512 * 4)).reshape(k // 512, 4)
    idx = np.arange(k)
    return np.exp2(a[idx // 512, idx % 128 // 32])


BF16 = ml_dtypes.bfloat16


def bf(x):
    return np.asarray(x, np.float32).astype(BF16)


def f64(x):
    return np.asarray(x).astype(np.float64)


B, D_IN, D_HID, D_OUT, LAT = 8192, 192, 512, 256, 16
BN_EPS = 1e-5
L2_EPS = 1e-12


def setup_inputs():
    t = mx_kscale(D_HID)
    col_sd = np.exp(0.4 * np.random.standard_normal(D_HID))
    col_mean = 0.5 * np.random.standard_normal(D_HID)
    return {
        "y_lin": bf(np.random.standard_normal((B, D_HID)) * col_sd + col_mean),
        "gamma": bf((1.0 + 0.2 * np.random.standard_normal(D_HID)) * t),
        "beta": bf(0.3 * np.random.standard_normal(D_HID) * t),
        "W2": bf(np.random.standard_normal((D_OUT, D_HID)) / np.sqrt(D_HID) / t[None, :]),
        "b2": bf(0.2 * np.random.standard_normal(D_OUT)),
    }


def reference(y_lin, gamma, beta, W2, b2):
    y = f64(y_lin)
    mean = np.mean(y, axis=0)
    var = np.mean((y - mean) ** 2, axis=0)
    y = (y - mean) * (1.0 / np.sqrt(var + BN_EPS)) * f64(gamma) + f64(beta)
    a = np.maximum(y, 0.0)
    p = (mxq(a, 1, "e4m3") @ mxq(f64(W2), 1, "e4m3").T) + f64(b2)
    n = np.sqrt(np.sum(p * p, axis=1, keepdims=True))
    return p / np.maximum(n, L2_EPS)

@@ -1,0 +1,256 @@
+from contextlib import ExitStack
+
+import concourse.mybir as mybir
+from concourse.masks import make_identity
+
+FLOPS = 2 * 8192 * 512 * 256
+
+FP8X4 = mybir.dt.float8_e4m3fn_x4
+BF16 = mybir.dt.bfloat16
+F32 = mybir.dt.float32
+U32 = mybir.dt.uint32
+U8 = mybir.dt.uint8
+ALU = mybir.AluOpType
+ACT = mybir.ActivationFunctionType
+AX = mybir.AxisListType
+
+P = 128
+B = 8192
+K = 512
+O = 256
+T = K // P
+G = B // P
+UNIT = 4
+NU = G // UNIT
+UC = UNIT * P
+SP = 3
+BN_EPS = 1e-5
+L2_EPS = 1e-12
+LOAD_BOUNDS = [0, 4, 8, 16, 24, 32, 40, 48, 56, 64]
+CHUNKS = [8, 8, 8, 8, 8, 8, 8, 4, 4]
+S_SHARE = 4
+
+
+def tile_simclr_pa_t_kernel(tc, y_lin, gamma, beta, W2, b2, out):
+    nc = tc.nc
+    yv = y_lin.rearrange("(p g) k -> p g k", g=G)
+    ov = out.rearrange("(p g) o -> p g o", g=G)
+    with ExitStack() as ctx:
+        const = ctx.enter_context(tc.tile_pool(name="const", bufs=1))
+        XT = const.tile([P, T, B], BF16, name="XT")
+        one1 = const.tile([P, 1], F32, name="one1")
+        warm = const.tile([P, 1], F32, name="warm")
+        eps = const.tile([P, 1], F32, name="eps")
+        ident = const.tile([P, P], BF16, name="ident")
+        ones = const.tile([P, P], BF16, name="ones")
+        gb = const.tile([P, P], BF16, name="gb")
+        gbT = const.tile([P, 2 * T], F32, name="gbT")
+        b2z = const.tile([P, O], BF16, name="b2z")
+        b2b = const.tile([P, 2, O], F32, name="b2b")
+        w_sb = const.tile([P, 2, K], BF16, name="w_sb")
+        wg = const.tile([P, O, T], BF16, name="wg", align_bytes=64)
+        w_codes = const.tile([P, O], U32, name="w_codes", align_bytes=64)
+        w_scales = const.tile([P, O], U8, name="w_scales", align_bytes=64)
+        negm0 = const.tile([P, SP], F32, name="negm0")
+        sq = const.tile([P, SP * NU], F32, name="sq")
+        st = const.tile([P, NU, 6], F32, name="st")
+        mv = const.tile([P, T, 2], F32, name="mv")
+        sxs = const.tile([P, SP], F32, name="sxs")
+        sqs = const.tile([P, SP], F32, name="sqs")
+        dm = const.tile([P, SP], F32, name="dm")
+        dm2 = const.tile([P, SP], F32, name="dm2")
+        std = const.tile([P, T], F32, name="std")
+        rstd = const.tile([P, T], F32, name="rstd")
+        sc = const.tile([P, T], F32, name="sc")
+        ms = const.tile([P, T], F32, name="ms")
+        sh = const.tile([P, T], F32, name="sh")
+
+        nc.vector.memset(one1[:], 1.0)
+        nc.scalar.activation(out=warm[:], in_=one1[:], func=ACT.Sqrt)
+        nc.vector.memset(eps[:], BN_EPS)
+        nc.vector.memset(gb[:], 0.0)
+        nc.vector.memset(b2z[:], 0.0)
+        nc.vector.memset(ones[:], 1.0)
+        make_identity(nc, ident[:])
+        nc.scalar.dma_start(out=gb[0:T, :], in_=gamma.rearrange("(t p) -> t p", p=P))
+        nc.scalar.dma_start(out=gb[T : 2 * T, :], in_=beta.rearrange("(t p) -> t p", p=P))
+        nc.scalar.dma_start(out=b2z[0:1, :], in_=b2.rearrange("(a o) -> a o", a=1))
+
+        with ExitStack() as ph1:
+            ypool = ph1.enter_context(tc.tile_pool(name="ypool", bufs=1))
+            jpool = ph1.enter_context(tc.tile_pool(name="jpool", bufs=2))
+            pss = ph1.enter_context(tc.psum_pool(name="pss", bufs=1))
+            pst = ph1.enter_context(tc.psum_pool(name="pst", bufs=6))
+            Y = ypool.tile([P, G, K], BF16, name="Y")
+            sx_ps = pss.tile([P, SP * NU], F32, name="sx_ps")
+            for i in range(len(LOAD_BOUNDS) - 1):
+                g0, g1 = LOAD_BOUNDS[i], LOAD_BOUNDS[i + 1]
+                nc.sync.dma_start(out=Y[:, g0:g1, :], in_=yv[:, g0:g1, :])
+                if i == 1:
+                    nc.sync.dma_start(out=w_sb[:], in_=W2.rearrange("(h o) k -> o h k", o=P))
+
+            gb_ps = pss.tile([P, P], BF16, tag="setup")
+            nc.tensor.transpose(gb_ps[:], gb[:], ident[:])
+            nc.scalar.copy(out=gbT[:], in_=gb_ps[:, 0 : 2 * T])
+            b2_ps = pss.tile([P, O], F32, tag="setup")
+            nc.tensor.matmul(out=b2_ps[:], lhsT=ones[:], rhs=b2z[:], start=True, stop=True)
+            for h in range(2):
+                nc.scalar.copy(out=b2b[:, h, :], in_=b2_ps[:])
+            m0_ps = pss.tile([P, SP], F32, tag="setup")
+            for t in range(SP):
+                nc.tensor.matmul(
+                    out=m0_ps[:, t : t + 1],
+                    lhsT=Y[:, 0, t * P : (t + 1) * P],
+                    rhs=ones[:, 0:1],
+                    start=True,
+                    stop=True,
+                )
+            nc.scalar.activation(out=negm0[:], in_=m0_ps[:], func=ACT.Copy, scale=-1.0 / P)
+
+            for q in range(NU):
+                cols = slice(q * UC, (q + 1) * UC)
+                for t in range(T):
+                    tp = pst.tile([P, UC], BF16, tag="tp")
+                    for j in range(UNIT):
+                        nc.tensor.transpose(
+                            tp[:, j * P : (j + 1) * P],
+                            Y[:, q * UNIT + j, t * P : (t + 1) * P],
+                            ident[:],
+                        )
+                    nc.vector.tensor_copy(out=XT[:, t, cols], in_=tp[:])
+                for t in range(SP):
+                    col = t * NU + q
+                    for j in range(UNIT):
+                        nc.tensor.matmul(
+                            out=sx_ps[:, col : col + 1],
+                            lhsT=Y[:, q * UNIT + j, t * P : (t + 1) * P],
+                            rhs=ones[:, 0:1],
+                            start=(j == 0),
+                            stop=(j == UNIT - 1),
+                        )
+                    junk = jpool.tile([P, UC], BF16, tag="junk")
+                    nc.scalar.activation(
+                        out=junk[:],
+                        in_=XT[:, t, cols],
+                        func=ACT.Square,
+                        bias=negm0[:, t : t + 1],
+                        accum_out=sq[:, col : col + 1],
+                    )
+                if q == 2:
+                    wt_ps = pss.tile([P, T, O], BF16, tag="setup")
+                    for t in range(T):
+                        for h in range(2):
+                            nc.tensor.transpose(
+                                wt_ps[:, t, h * P : (h + 1) * P],
+                                w_sb[:, h, t * P : (t + 1) * P],
+                                ident[:],
+                            )
+                    nc.vector.tensor_copy(out=wg[:], in_=wt_ps[:].rearrange("p t o -> p o t"))
+            for q in range(NU):
+                nc.vector.bn_stats(out=st[:, q, :], in_=XT[:, SP, q * UC : (q + 1) * UC])
+            nc.vector.quantize_mx(
+                out=w_codes[:].bitcast(FP8X4),
+                scales=w_scales[:],
+                in_=wg[:].rearrange("p o t -> p (o t)"),
+            )
+
+            nc.vector.bn_aggr(out=mv[:, SP, :], in_=st[:].rearrange("p q s -> p (q s)"))
+            nc.vector.tensor_reduce(
+                out=sxs[:], in_=sx_ps[:].rearrange("p (t q) -> p t q", q=NU), axis=AX.X, op=ALU.add
+            )
+            nc.vector.tensor_reduce(
+                out=sqs[:], in_=sq[:].rearrange("p (t q) -> p t q", q=NU), axis=AX.X, op=ALU.add
+            )
+            nc.vector.scalar_tensor_tensor(
+                out=dm[:], in0=sxs[:], scalar=1.0 / B, in1=negm0[:], op0=ALU.mult, op1=ALU.add
+            )
+            nc.vector.tensor_tensor(out=dm2[:], in0=dm[:], in1=dm[:], op=ALU.mult)
+            nc.vector.scalar_tensor_tensor(
+                out=mv[:, 0:SP, 1], in0=sqs[:], scalar=1.0 / B, in1=dm2[:], op0=ALU.mult, op1=ALU.subtract
+            )
+            nc.vector.tensor_tensor(out=mv[:, 0:SP, 0], in0=dm[:], in1=negm0[:], op=ALU.subtract)
+            nc.scalar.activation(out=std[:], in_=mv[:, :, 1], func=ACT.Sqrt, bias=eps[:, 0:1])
+            nc.vector.reciprocal(out=rstd[:], in_=std[:])
+            nc.vector.tensor_tensor(out=sc[:], in0=gbT[:, 0:T], in1=rstd[:], op=ALU.mult)
+            nc.vector.tensor_tensor(out=ms[:], in0=mv[:, :, 0], in1=sc[:], op=ALU.mult)
+            nc.vector.tensor_tensor(out=sh[:], in0=gbT[:, T : 2 * T], in1=ms[:], op=ALU.subtract)
+
+        zpool = ctx.enter_context(tc.tile_pool(name="zpool", bufs=2))
+        gpool = ctx.enter_context(tc.tile_pool(name="gpool", bufs=3))
+        qpool = ctx.enter_context(tc.tile_pool(name="qpool", bufs=3))
+        ppool = ctx.enter_context(tc.tile_pool(name="ppool", bufs=4))
+        spool = ctx.enter_context(tc.tile_pool(name="spool", bufs=4))
+        kpool = ctx.enter_context(tc.tile_pool(name="kpool", bufs=2))
+        psm = ctx.enter_context(tc.psum_pool(name="psm", bufs=8))
+        CMAX = max(CHUNKS)
+        g0 = 0
+        for ng in CHUNKS:
+            n = ng * P
+            c0 = g0 * P
+            cv = n - n // S_SHARE
+            Z = zpool.tile([P, T, CMAX * P], BF16, tag="Z")
+            for t in range(T):
+                nc.vector.tensor_scalar(
+                    out=Z[:, t, 0:n],
+                    in0=XT[:, t, c0 : c0 + n],
+                    scalar1=sc[:, t : t + 1],
+                    scalar2=sh[:, t : t + 1],
+                    op0=ALU.mult,
+                    op1=ALU.add,
+                )
+            Gt = gpool.tile([P, CMAX * P, T], BF16, tag="Gt", align_bytes=64)
+            nc.vector.tensor_scalar(
+                out=Gt[:, 0:cv, :].rearrange("p (c i) t -> p c t i", i=4),
+                in0=Z[:, :, 0:cv].rearrange("p t (c i) -> p c t i", i=4),
+                scalar1=0.0,
+                scalar2=None,
+                op0=ALU.max,
+            )
+            nc.scalar.activation(
+                out=Gt[:, cv:n, :].rearrange("p (c i) t -> p c t i", i=4),
+                in_=Z[:, :, cv:n].rearrange("p t (c i) -> p c t i", i=4),
+                func=ACT.Relu,
+            )
+            codes = qpool.tile([P, CMAX * P], U32, tag="codes", align_bytes=64)
+            scales = qpool.tile([P, CMAX * P], U8, tag="scales", align_bytes=64)
+            nc.vector.quantize_mx(
+                out=codes[:, 0:n].bitcast(FP8X4),
+                scales=scales[:, 0:n],
+                in_=Gt[:, 0:n, :].rearrange("p b t -> p (b t)"),
+            )
+            Pt = ppool.tile([P, CMAX, O], F32, tag="Pt")
+            ss = spool.tile([P, CMAX], F32, tag="ss")
+            ssc = spool.tile([P, CMAX], F32, tag="ssc")
+            nrm = spool.tile([P, CMAX], F32, tag="nrm")
+            rinv = spool.tile([P, CMAX], F32, tag="rinv")
+            for i in range(ng // 2):
+                acc = psm.tile([P, 2, O], F32, tag="acc")
+                for h in range(2):
+                    m = slice((2 * i + h) * P, (2 * i + h + 1) * P)
+                    nc.tensor.matmul_mx(
+                        out=acc[:, h, :],
+                        lhsT=codes[:, m].bitcast(FP8X4),
+                        lhsT_scale=scales[:, m],
+                        rhs=w_codes[:].bitcast(FP8X4),
+                        rhs_scale=w_scales[:],
+                        start=True,
+                        stop=True,
+                    )
+                nc.vector.tensor_tensor(out=Pt[:, 2 * i : 2 * i + 2, :], in0=acc[:], in1=b2b[:], op=ALU.add)
+                for h in range(2):
+                    r = 2 * i + h
+                    junk2 = kpool.tile([P, O], BF16, tag="junk2")
+                    nc.scalar.activation(
+                        out=junk2[:], in_=Pt[:, r, :], func=ACT.Square, accum_out=ss[:, r : r + 1]
+                    )
+            nc.vector.tensor_scalar(
+                out=ssc[:, 0:ng], in0=ss[:, 0:ng], scalar1=L2_EPS * L2_EPS, scalar2=None, op0=ALU.max
+            )
+            nc.scalar.activation(out=nrm[:, 0:ng], in_=ssc[:, 0:ng], func=ACT.Sqrt)
+            nc.vector.reciprocal(out=rinv[:, 0:ng], in_=nrm[:, 0:ng])
+            for r in range(ng):
+                nc.scalar.activation(
+                    out=Pt[:, r, :], in_=Pt[:, r, :], func=ACT.Copy, scale=rinv[:, r : r + 1]
+                )
+            nc.sync.dma_start(out=ov[:, g0 : g0 + ng, :], in_=Pt[:, 0:ng, :])
+            g0 += ng

@@ -27,8 +27,12 @@ SP = 3
 BN_EPS = 1e-5
 L2_EPS = 1e-12
 LOAD_BOUNDS = [0, 4, 8, 16, 24, 32, 40, 48, 56, 64]
+SPAN = 2
+SUMQ = 4
+SUMN = 24
+WARM = 5
 CHUNKS = [8, 8, 8, 8, 8, 8, 8, 4, 4]
-S_SHARE = 4
+V_SCALE = 2
 
 
 def tile_simclr_pa_t_kernel(tc, y_lin, gamma, beta, W2, b2, out):
@@ -36,13 +40,16 @@ def tile_simclr_pa_t_kernel(tc, y_lin, gamma, beta, W2, b2, out):
     yv = y_lin.rearrange("(p g) k -> p g k", g=G)
     ov = out.rearrange("(p g) o -> p g o", g=G)
     with ExitStack() as ctx:
+        ctx.enter_context(tc.manual_schedule())
         const = ctx.enter_context(tc.tile_pool(name="const", bufs=1))
         XT = const.tile([P, T, B], BF16, name="XT")
         one1 = const.tile([P, 1], F32, name="one1")
         warm = const.tile([P, 1], F32, name="warm")
         eps = const.tile([P, 1], F32, name="eps")
+        tiny = const.tile([P, 1], F32, name="tiny")
         ident = const.tile([P, P], BF16, name="ident")
         ones = const.tile([P, P], BF16, name="ones")
+        wf = const.tile([P, P], F32, name="wf")
         gb = const.tile([P, P], BF16, name="gb")
         gbT = const.tile([P, 2 * T], F32, name="gbT")
         b2z = const.tile([P, O], BF16, name="b2z")
@@ -52,7 +59,8 @@ def tile_simclr_pa_t_kernel(tc, y_lin, gamma, beta, W2, b2, out):
         w_codes = const.tile([P, O], U32, name="w_codes", align_bytes=64)
         w_scales = const.tile([P, O], U8, name="w_scales", align_bytes=64)
         negm0 = const.tile([P, SP], F32, name="negm0")
-        sq = const.tile([P, SP * NU], F32, name="sq")
+        NS = NU // SPAN
+        sq = const.tile([P, SP * NS], F32, name="sq")
         st = const.tile([P, NU, 6], F32, name="st")
         mv = const.tile([P, T, 2], F32, name="mv")
         sxs = const.tile([P, SP], F32, name="sxs")
@@ -65,16 +73,18 @@ def tile_simclr_pa_t_kernel(tc, y_lin, gamma, beta, W2, b2, out):
         ms = const.tile([P, T], F32, name="ms")
         sh = const.tile([P, T], F32, name="sh")
 
-        nc.vector.memset(one1[:], 1.0)
-        nc.scalar.activation(out=warm[:], in_=one1[:], func=ACT.Sqrt)
-        nc.vector.memset(eps[:], BN_EPS)
+        nc.vector.memset(wf[:], 1.0)
         nc.vector.memset(gb[:], 0.0)
         nc.vector.memset(b2z[:], 0.0)
-        nc.vector.memset(ones[:], 1.0)
-        make_identity(nc, ident[:])
         nc.scalar.dma_start(out=gb[0:T, :], in_=gamma.rearrange("(t p) -> t p", p=P))
         nc.scalar.dma_start(out=gb[T : 2 * T, :], in_=beta.rearrange("(t p) -> t p", p=P))
         nc.scalar.dma_start(out=b2z[0:1, :], in_=b2.rearrange("(a o) -> a o", a=1))
+        nc.vector.memset(one1[:], 1.0)
+        nc.scalar.activation(out=warm[:], in_=one1[:], func=ACT.Sqrt)
+        nc.vector.memset(ones[:], 1.0)
+        nc.vector.memset(eps[:], BN_EPS)
+        nc.vector.memset(tiny[:], 1e-30)
+        make_identity(nc, ident[:])
 
         with ExitStack() as ph1:
             ypool = ph1.enter_context(tc.tile_pool(name="ypool", bufs=1))
@@ -82,20 +92,16 @@ def tile_simclr_pa_t_kernel(tc, y_lin, gamma, beta, W2, b2, out):
             pss = ph1.enter_context(tc.psum_pool(name="pss", bufs=1))
             pst = ph1.enter_context(tc.psum_pool(name="pst", bufs=6))
             Y = ypool.tile([P, G, K], BF16, name="Y")
-            sx_ps = pss.tile([P, SP * NU], F32, name="sx_ps")
+            sx_ps = pss.tile([P, (NU // SUMQ) * SP * SUMN], F32, name="sx_ps")
+            warm_ps = pss.tile([P, P], F32, tag="setup")
+            for i in range(WARM):
+                nc.tensor.matmul(out=warm_ps[:], lhsT=wf[:], rhs=wf[:], start=True, stop=True)
             for i in range(len(LOAD_BOUNDS) - 1):
                 g0, g1 = LOAD_BOUNDS[i], LOAD_BOUNDS[i + 1]
                 nc.sync.dma_start(out=Y[:, g0:g1, :], in_=yv[:, g0:g1, :])
                 if i == 1:
                     nc.sync.dma_start(out=w_sb[:], in_=W2.rearrange("(h o) k -> o h k", o=P))
 
-            gb_ps = pss.tile([P, P], BF16, tag="setup")
-            nc.tensor.transpose(gb_ps[:], gb[:], ident[:])
-            nc.scalar.copy(out=gbT[:], in_=gb_ps[:, 0 : 2 * T])
-            b2_ps = pss.tile([P, O], F32, tag="setup")
-            nc.tensor.matmul(out=b2_ps[:], lhsT=ones[:], rhs=b2z[:], start=True, stop=True)
-            for h in range(2):
-                nc.scalar.copy(out=b2b[:, h, :], in_=b2_ps[:])
             m0_ps = pss.tile([P, SP], F32, tag="setup")
             for t in range(SP):
                 nc.tensor.matmul(
@@ -118,24 +124,32 @@ def tile_simclr_pa_t_kernel(tc, y_lin, gamma, beta, W2, b2, out):
                             ident[:],
                         )
                     nc.vector.tensor_copy(out=XT[:, t, cols], in_=tp[:])
-                for t in range(SP):
-                    col = t * NU + q
-                    for j in range(UNIT):
-                        nc.tensor.matmul(
-                            out=sx_ps[:, col : col + 1],
-                            lhsT=Y[:, q * UNIT + j, t * P : (t + 1) * P],
-                            rhs=ones[:, 0:1],
-                            start=(j == 0),
-                            stop=(j == UNIT - 1),
+                if q > 0:
+                    nc.vector.bn_stats(out=st[:, q - 1, :], in_=XT[:, SP, (q - 1) * UC : q * UC])
+                if q % SUMQ == SUMQ - 1:
+                    blk = q // SUMQ
+                    ng = SUMQ * UNIT
+                    for t in range(SP):
+                        col = (blk * SP + t) * SUMN
+                        for j in range(ng):
+                            nc.tensor.matmul(
+                                out=sx_ps[:, col : col + SUMN],
+                                lhsT=Y[:, blk * ng + j, t * P : (t + 1) * P],
+                                rhs=ones[:, 0:SUMN],
+                                start=(j == 0),
+                                stop=(j == ng - 1),
+                            )
+                if q % SPAN == SPAN - 1:
+                    v = q // SPAN
+                    for t in range(SP):
+                        junk = jpool.tile([P, SPAN * UC], BF16, tag="junk")
+                        nc.scalar.activation(
+                            out=junk[:],
+                            in_=XT[:, t, v * SPAN * UC : (v + 1) * SPAN * UC],
+                            func=ACT.Square,
+                            bias=negm0[:, t : t + 1],
+                            accum_out=sq[:, t * NS + v : t * NS + v + 1],
                         )
-                    junk = jpool.tile([P, UC], BF16, tag="junk")
-                    nc.scalar.activation(
-                        out=junk[:],
-                        in_=XT[:, t, cols],
-                        func=ACT.Square,
-                        bias=negm0[:, t : t + 1],
-                        accum_out=sq[:, col : col + 1],
-                    )
                 if q == 2:
                     wt_ps = pss.tile([P, T, O], BF16, tag="setup")
                     for t in range(T):
@@ -146,29 +160,38 @@ def tile_simclr_pa_t_kernel(tc, y_lin, gamma, beta, W2, b2, out):
                                 ident[:],
                             )
                     nc.vector.tensor_copy(out=wg[:], in_=wt_ps[:].rearrange("p t o -> p o t"))
-            for q in range(NU):
-                nc.vector.bn_stats(out=st[:, q, :], in_=XT[:, SP, q * UC : (q + 1) * UC])
-            nc.vector.quantize_mx(
-                out=w_codes[:].bitcast(FP8X4),
-                scales=w_scales[:],
-                in_=wg[:].rearrange("p o t -> p (o t)"),
-            )
-
+                if q == 3:
+                    gb_ps = pss.tile([P, P], BF16, tag="setup")
+                    nc.tensor.transpose(gb_ps[:], gb[:], ident[:])
+                    nc.scalar.copy(out=gbT[:], in_=gb_ps[:, 0 : 2 * T])
+                    b2_ps = pss.tile([P, O], F32, tag="setup")
+                    nc.tensor.matmul(out=b2_ps[:], lhsT=ones[:], rhs=b2z[:], start=True, stop=True)
+                    for h in range(2):
+                        nc.scalar.copy(out=b2b[:, h, :], in_=b2_ps[:])
+            nc.vector.bn_stats(out=st[:, NU - 1, :], in_=XT[:, SP, (NU - 1) * UC : NU * UC])
             nc.vector.bn_aggr(out=mv[:, SP, :], in_=st[:].rearrange("p q s -> p (q s)"))
             nc.vector.tensor_reduce(
-                out=sxs[:], in_=sx_ps[:].rearrange("p (t q) -> p t q", q=NU), axis=AX.X, op=ALU.add
-            )
-            nc.vector.tensor_reduce(
-                out=sqs[:], in_=sq[:].rearrange("p (t q) -> p t q", q=NU), axis=AX.X, op=ALU.add
+                out=sxs[:],
+                in_=sx_ps[:].rearrange("p (k t n) -> p t k n", t=SP, n=SUMN)[:, :, :, 0],
+                axis=AX.X,
+                op=ALU.add,
             )
             nc.vector.scalar_tensor_tensor(
                 out=dm[:], in0=sxs[:], scalar=1.0 / B, in1=negm0[:], op0=ALU.mult, op1=ALU.add
             )
             nc.vector.tensor_tensor(out=dm2[:], in0=dm[:], in1=dm[:], op=ALU.mult)
+            nc.vector.tensor_tensor(out=mv[:, 0:SP, 0], in0=dm[:], in1=negm0[:], op=ALU.subtract)
+            nc.vector.quantize_mx(
+                out=w_codes[:].bitcast(FP8X4),
+                scales=w_scales[:],
+                in_=wg[:].rearrange("p o t -> p (o t)"),
+            )
+            nc.vector.tensor_reduce(
+                out=sqs[:], in_=sq[:].rearrange("p (t v) -> p t v", v=NS), axis=AX.X, op=ALU.add
+            )
             nc.vector.scalar_tensor_tensor(
                 out=mv[:, 0:SP, 1], in0=sqs[:], scalar=1.0 / B, in1=dm2[:], op0=ALU.mult, op1=ALU.subtract
             )
-            nc.vector.tensor_tensor(out=mv[:, 0:SP, 0], in0=dm[:], in1=negm0[:], op=ALU.subtract)
             nc.scalar.activation(out=std[:], in_=mv[:, :, 1], func=ACT.Sqrt, bias=eps[:, 0:1])
             nc.vector.reciprocal(out=rstd[:], in_=std[:])
             nc.vector.tensor_tensor(out=sc[:], in0=gbT[:, 0:T], in1=rstd[:], op=ALU.mult)
@@ -183,74 +206,121 @@ def tile_simclr_pa_t_kernel(tc, y_lin, gamma, beta, W2, b2, out):
         kpool = ctx.enter_context(tc.tile_pool(name="kpool", bufs=2))
         psm = ctx.enter_context(tc.psum_pool(name="psm", bufs=8))
         CMAX = max(CHUNKS)
-        g0 = 0
-        for ng in CHUNKS:
-            n = ng * P
-            c0 = g0 * P
-            cv = n - n // S_SHARE
-            Z = zpool.tile([P, T, CMAX * P], BF16, tag="Z")
+        NCH = len(CHUNKS)
+        starts = [sum(CHUNKS[:c]) for c in range(NCH)]
+        Zs, Gs, Cs, Ss, As, Ps, SSs, RIs = {}, {}, {}, {}, {}, {}, {}, {}
+
+        def affine(c):
+            n = CHUNKS[c] * P
+            c0 = starts[c] * P
+            Zs[c] = zpool.tile([P, T, CMAX * P], BF16, tag="Z", name="Z")
             for t in range(T):
                 nc.vector.tensor_scalar(
-                    out=Z[:, t, 0:n],
+                    out=Zs[c][:, t, 0:n],
                     in0=XT[:, t, c0 : c0 + n],
                     scalar1=sc[:, t : t + 1],
                     scalar2=sh[:, t : t + 1],
                     op0=ALU.mult,
                     op1=ALU.add,
                 )
-            Gt = gpool.tile([P, CMAX * P, T], BF16, tag="Gt", align_bytes=64)
+
+        def regroup(c):
+            n = CHUNKS[c] * P
+            cv = n - (n // 2 if c < 2 else 3 * n // 8)
+            Gs[c] = gpool.tile([P, CMAX * P, T], BF16, tag="Gt", name="Gt", align_bytes=64)
             nc.vector.tensor_scalar(
-                out=Gt[:, 0:cv, :].rearrange("p (c i) t -> p c t i", i=4),
-                in0=Z[:, :, 0:cv].rearrange("p t (c i) -> p c t i", i=4),
+                out=Gs[c][:, 0:cv, :].rearrange("p (c i) t -> p c t i", i=4),
+                in0=Zs[c][:, :, 0:cv].rearrange("p t (c i) -> p c t i", i=4),
                 scalar1=0.0,
                 scalar2=None,
                 op0=ALU.max,
             )
-            nc.scalar.activation(
-                out=Gt[:, cv:n, :].rearrange("p (c i) t -> p c t i", i=4),
-                in_=Z[:, :, cv:n].rearrange("p t (c i) -> p c t i", i=4),
-                func=ACT.Relu,
-            )
-            codes = qpool.tile([P, CMAX * P], U32, tag="codes", align_bytes=64)
-            scales = qpool.tile([P, CMAX * P], U8, tag="scales", align_bytes=64)
+            if cv < n:
+                nc.scalar.activation(
+                    out=Gs[c][:, cv:n, :].rearrange("p (c i) t -> p c t i", i=4),
+                    in_=Zs[c][:, :, cv:n].rearrange("p t (c i) -> p c t i", i=4),
+                    func=ACT.Relu,
+                )
+
+        def quantise_multiply(c):
+            n = CHUNKS[c] * P
+            Cs[c] = qpool.tile([P, CMAX * P], U32, tag="codes", name="codes", align_bytes=64)
+            Ss[c] = qpool.tile([P, CMAX * P], U8, tag="scales", name="scales", align_bytes=64)
             nc.vector.quantize_mx(
-                out=codes[:, 0:n].bitcast(FP8X4),
-                scales=scales[:, 0:n],
-                in_=Gt[:, 0:n, :].rearrange("p b t -> p (b t)"),
+                out=Cs[c][:, 0:n].bitcast(FP8X4),
+                scales=Ss[c][:, 0:n],
+                in_=Gs[c][:, 0:n, :].rearrange("p b t -> p (b t)"),
             )
-            Pt = ppool.tile([P, CMAX, O], F32, tag="Pt")
-            ss = spool.tile([P, CMAX], F32, tag="ss")
-            ssc = spool.tile([P, CMAX], F32, tag="ssc")
-            nrm = spool.tile([P, CMAX], F32, tag="nrm")
-            rinv = spool.tile([P, CMAX], F32, tag="rinv")
-            for i in range(ng // 2):
-                acc = psm.tile([P, 2, O], F32, tag="acc")
+            As[c] = []
+            for i in range(CHUNKS[c] // 2):
+                acc = psm.tile([P, 2, O], F32, tag="acc", name="acc")
+                As[c].append(acc)
                 for h in range(2):
                     m = slice((2 * i + h) * P, (2 * i + h + 1) * P)
                     nc.tensor.matmul_mx(
                         out=acc[:, h, :],
-                        lhsT=codes[:, m].bitcast(FP8X4),
-                        lhsT_scale=scales[:, m],
+                        lhsT=Cs[c][:, m].bitcast(FP8X4),
+                        lhsT_scale=Ss[c][:, m],
                         rhs=w_codes[:].bitcast(FP8X4),
                         rhs_scale=w_scales[:],
                         start=True,
                         stop=True,
                     )
-                nc.vector.tensor_tensor(out=Pt[:, 2 * i : 2 * i + 2, :], in0=acc[:], in1=b2b[:], op=ALU.add)
-                for h in range(2):
-                    r = 2 * i + h
-                    junk2 = kpool.tile([P, O], BF16, tag="junk2")
-                    nc.scalar.activation(
-                        out=junk2[:], in_=Pt[:, r, :], func=ACT.Square, accum_out=ss[:, r : r + 1]
-                    )
-            nc.vector.tensor_scalar(
-                out=ssc[:, 0:ng], in0=ss[:, 0:ng], scalar1=L2_EPS * L2_EPS, scalar2=None, op0=ALU.max
-            )
-            nc.scalar.activation(out=nrm[:, 0:ng], in_=ssc[:, 0:ng], func=ACT.Sqrt)
-            nc.vector.reciprocal(out=rinv[:, 0:ng], in_=nrm[:, 0:ng])
-            for r in range(ng):
-                nc.scalar.activation(
-                    out=Pt[:, r, :], in_=Pt[:, r, :], func=ACT.Copy, scale=rinv[:, r : r + 1]
+
+        def bias_squares(c):
+            ng = CHUNKS[c]
+            Ps[c] = ppool.tile([P, CMAX, O], F32, tag="Pt", name="Pt")
+            SSs[c] = spool.tile([P, CMAX], F32, tag="ss", name="ss")
+            for i in range(ng // 2):
+                nc.vector.tensor_tensor(
+                    out=Ps[c][:, 2 * i : 2 * i + 2, :], in0=As[c][i][:], in1=b2b[:], op=ALU.add
                 )
-            nc.sync.dma_start(out=ov[:, g0 : g0 + ng, :], in_=Pt[:, 0:ng, :])
-            g0 += ng
+            for r in range(ng):
+                junk2 = kpool.tile([P, O], BF16, tag="junk2")
+                nc.scalar.activation(
+                    out=junk2[:], in_=Ps[c][:, r, :], func=ACT.Square, accum_out=SSs[c][:, r : r + 1]
+                )
+            nrm = spool.tile([P, CMAX], F32, tag="nrm")
+            nc.scalar.activation(out=nrm[:, 0:ng], in_=SSs[c][:, 0:ng], func=ACT.Sqrt, bias=tiny[:, 0:1])
+            SSs[c] = nrm
+
+        def inverse_norm(c):
+            ng = CHUNKS[c]
+            nrc = spool.tile([P, CMAX], F32, tag="nrc")
+            RIs[c] = spool.tile([P, CMAX], F32, tag="rinv", name="rinv")
+            nc.vector.tensor_scalar(
+                out=nrc[:, 0:ng], in0=SSs[c][:, 0:ng], scalar1=L2_EPS, scalar2=None, op0=ALU.max
+            )
+            nc.vector.reciprocal(out=RIs[c][:, 0:ng], in_=nrc[:, 0:ng])
+
+        def scale_store(c):
+            ng = CHUNKS[c]
+            for r in range(ng):
+                if r < V_SCALE:
+                    nc.vector.tensor_scalar(
+                        out=Ps[c][:, r, :],
+                        in0=Ps[c][:, r, :],
+                        scalar1=RIs[c][:, r : r + 1],
+                        scalar2=None,
+                        op0=ALU.mult,
+                    )
+                else:
+                    nc.scalar.activation(
+                        out=Ps[c][:, r, :], in_=Ps[c][:, r, :], func=ACT.Copy, scale=RIs[c][:, r : r + 1]
+                    )
+            nc.sync.dma_start(out=ov[:, starts[c] : starts[c] + ng, :], in_=Ps[c][:, 0:ng, :])
+
+        affine(0)
+        for i in range(NCH + 2):
+            if 0 <= i - 2:
+                inverse_norm(i - 2)
+            if i < NCH:
+                regroup(i)
+            if 0 <= i - 2:
+                scale_store(i - 2)
+            if i + 1 < NCH:
+                affine(i + 1)
+            if 0 <= i - 1 < NCH:
+                bias_squares(i - 1)
+            if i < NCH:
+                quantise_multiply(i)

@@ -29,8 +29,9 @@ L2_EPS = 1e-12
 LOAD_BOUNDS = [0, 4, 8, 16, 24, 32, 40, 48, 56, 64]
 SPAN = 2
 SUMQ = 4
-SUMN = 24
-WARM = 5
+SUMN = 1
+WARM = 8
+PUMP = 256
 CHUNKS = [8, 8, 8, 8, 8, 8, 8, 4, 4]
 V_SCALE = 2
 
@@ -49,7 +50,7 @@ def tile_simclr_pa_t_kernel(tc, y_lin, gamma, beta, W2, b2, out):
         tiny = const.tile([P, 1], F32, name="tiny")
         ident = const.tile([P, P], BF16, name="ident")
         ones = const.tile([P, P], BF16, name="ones")
-        wf = const.tile([P, P], F32, name="wf")
+        wf = const.tile([P, PUMP], F32, name="wf")
         gb = const.tile([P, P], BF16, name="gb")
         gbT = const.tile([P, 2 * T], F32, name="gbT")
         b2z = const.tile([P, O], BF16, name="b2z")
@@ -90,12 +91,12 @@ def tile_simclr_pa_t_kernel(tc, y_lin, gamma, beta, W2, b2, out):
             ypool = ph1.enter_context(tc.tile_pool(name="ypool", bufs=1))
             jpool = ph1.enter_context(tc.tile_pool(name="jpool", bufs=2))
             pss = ph1.enter_context(tc.psum_pool(name="pss", bufs=1))
-            pst = ph1.enter_context(tc.psum_pool(name="pst", bufs=6))
+            pst = ph1.enter_context(tc.psum_pool(name="pst", bufs=5))
             Y = ypool.tile([P, G, K], BF16, name="Y")
             sx_ps = pss.tile([P, (NU // SUMQ) * SP * SUMN], F32, name="sx_ps")
-            warm_ps = pss.tile([P, P], F32, tag="setup")
+            pump_ps = pss.tile([P, PUMP], F32, name="pump_ps")
             for i in range(WARM):
-                nc.tensor.matmul(out=warm_ps[:], lhsT=wf[:], rhs=wf[:], start=True, stop=True)
+                nc.tensor.matmul(out=pump_ps[:, 0:P], lhsT=wf[:, 0:P], rhs=wf[:, 0:P], start=True, stop=True)
             for i in range(len(LOAD_BOUNDS) - 1):
                 g0, g1 = LOAD_BOUNDS[i], LOAD_BOUNDS[i + 1]
                 nc.sync.dma_start(out=Y[:, g0:g1, :], in_=yv[:, g0:g1, :])
@@ -124,6 +125,7 @@ def tile_simclr_pa_t_kernel(tc, y_lin, gamma, beta, W2, b2, out):
                             ident[:],
                         )
                     nc.vector.tensor_copy(out=XT[:, t, cols], in_=tp[:])
+                nc.tensor.matmul(out=pump_ps[:], lhsT=wf[:, 0:P], rhs=wf[:], start=True, stop=True)
                 if q > 0:
                     nc.vector.bn_stats(out=st[:, q - 1, :], in_=XT[:, SP, (q - 1) * UC : q * UC])
                 if q % SUMQ == SUMQ - 1:

@@ -23,17 +23,13 @@ G = B // P
 UNIT = 4
 NU = G // UNIT
 UC = UNIT * P
-SP = 3
+SP = 2
+SUMQ = 4
 BN_EPS = 1e-5
 L2_EPS = 1e-12
 LOAD_BOUNDS = [0, 4, 8, 16, 24, 32, 40, 48, 56, 64]
-SPAN = 2
-SUMQ = 4
-SUMN = 1
-WARM = 8
-PUMP = 256
 CHUNKS = [8, 8, 8, 8, 8, 8, 8, 4, 4]
-V_SCALE = 2
+CMAX = 8
 
 
 def tile_simclr_pa_t_kernel(tc, y_lin, gamma, beta, W2, b2, out):
@@ -43,43 +39,46 @@ def tile_simclr_pa_t_kernel(tc, y_lin, gamma, beta, W2, b2, out):
     with ExitStack() as ctx:
         ctx.enter_context(tc.manual_schedule())
         const = ctx.enter_context(tc.tile_pool(name="const", bufs=1))
-        XT = const.tile([P, T, B], BF16, name="XT")
+        Y = const.tile([P, G, K], BF16, name="Y")
         one1 = const.tile([P, 1], F32, name="one1")
         warm = const.tile([P, 1], F32, name="warm")
         eps = const.tile([P, 1], F32, name="eps")
         tiny = const.tile([P, 1], F32, name="tiny")
         ident = const.tile([P, P], BF16, name="ident")
         ones = const.tile([P, P], BF16, name="ones")
-        wf = const.tile([P, PUMP], F32, name="wf")
         gb = const.tile([P, P], BF16, name="gb")
         gbT = const.tile([P, 2 * T], F32, name="gbT")
         b2z = const.tile([P, O], BF16, name="b2z")
         b2b = const.tile([P, 2, O], F32, name="b2b")
         w_sb = const.tile([P, 2, K], BF16, name="w_sb")
+        wt_sb = const.tile([P, T, O], BF16, name="wt_sb")
         wg = const.tile([P, O, T], BF16, name="wg", align_bytes=64)
         w_codes = const.tile([P, O], U32, name="w_codes", align_bytes=64)
         w_scales = const.tile([P, O], U8, name="w_scales", align_bytes=64)
         negm0 = const.tile([P, SP], F32, name="negm0")
-        NS = NU // SPAN
-        sq = const.tile([P, SP * NS], F32, name="sq")
-        st = const.tile([P, NU, 6], F32, name="st")
+        sq = const.tile([P, SP * NU], F32, name="sq")
+        st = const.tile([P, T - SP, NU, 6], F32, name="st")
         mv = const.tile([P, T, 2], F32, name="mv")
         sxs = const.tile([P, SP], F32, name="sxs")
         sqs = const.tile([P, SP], F32, name="sqs")
         dm = const.tile([P, SP], F32, name="dm")
         dm2 = const.tile([P, SP], F32, name="dm2")
+        nmg = const.tile([P, T], F32, name="nmg")
         std = const.tile([P, T], F32, name="std")
         rstd = const.tile([P, T], F32, name="rstd")
         sc = const.tile([P, T], F32, name="sc")
-        ms = const.tile([P, T], F32, name="ms")
         sh = const.tile([P, T], F32, name="sh")
 
-        nc.vector.memset(wf[:], 1.0)
         nc.vector.memset(gb[:], 0.0)
         nc.vector.memset(b2z[:], 0.0)
         nc.scalar.dma_start(out=gb[0:T, :], in_=gamma.rearrange("(t p) -> t p", p=P))
         nc.scalar.dma_start(out=gb[T : 2 * T, :], in_=beta.rearrange("(t p) -> t p", p=P))
         nc.scalar.dma_start(out=b2z[0:1, :], in_=b2.rearrange("(a o) -> a o", a=1))
+        for i in range(len(LOAD_BOUNDS) - 1):
+            g0, g1 = LOAD_BOUNDS[i], LOAD_BOUNDS[i + 1]
+            nc.sync.dma_start(out=Y[:, g0:g1, :], in_=yv[:, g0:g1, :])
+            if i == 1:
+                nc.sync.dma_start(out=w_sb[:], in_=W2.rearrange("(h o) k -> o h k", o=P))
         nc.vector.memset(one1[:], 1.0)
         nc.scalar.activation(out=warm[:], in_=one1[:], func=ACT.Sqrt)
         nc.vector.memset(ones[:], 1.0)
@@ -87,21 +86,17 @@ def tile_simclr_pa_t_kernel(tc, y_lin, gamma, beta, W2, b2, out):
         nc.vector.memset(tiny[:], 1e-30)
         make_identity(nc, ident[:])
 
+        def transposes(dst, g0, n, t):
+            for j in range(n):
+                nc.tensor.transpose(
+                    dst[:, j * P : (j + 1) * P], Y[:, g0 + j, t * P : (t + 1) * P], ident[:]
+                )
+
         with ExitStack() as ph1:
-            ypool = ph1.enter_context(tc.tile_pool(name="ypool", bufs=1))
             jpool = ph1.enter_context(tc.tile_pool(name="jpool", bufs=2))
             pss = ph1.enter_context(tc.psum_pool(name="pss", bufs=1))
-            pst = ph1.enter_context(tc.psum_pool(name="pst", bufs=5))
-            Y = ypool.tile([P, G, K], BF16, name="Y")
-            sx_ps = pss.tile([P, (NU // SUMQ) * SP * SUMN], F32, name="sx_ps")
-            pump_ps = pss.tile([P, PUMP], F32, name="pump_ps")
-            for i in range(WARM):
-                nc.tensor.matmul(out=pump_ps[:, 0:P], lhsT=wf[:, 0:P], rhs=wf[:, 0:P], start=True, stop=True)
-            for i in range(len(LOAD_BOUNDS) - 1):
-                g0, g1 = LOAD_BOUNDS[i], LOAD_BOUNDS[i + 1]
-                nc.sync.dma_start(out=Y[:, g0:g1, :], in_=yv[:, g0:g1, :])
-                if i == 1:
-                    nc.sync.dma_start(out=w_sb[:], in_=W2.rearrange("(h o) k -> o h k", o=P))
+            pst = ph1.enter_context(tc.psum_pool(name="pst", bufs=6))
+            sx_ps = pss.tile([P, (NU // SUMQ) * SP], F32, name="sx_ps")
 
             m0_ps = pss.tile([P, SP], F32, tag="setup")
             for t in range(SP):
@@ -115,43 +110,33 @@ def tile_simclr_pa_t_kernel(tc, y_lin, gamma, beta, W2, b2, out):
             nc.scalar.activation(out=negm0[:], in_=m0_ps[:], func=ACT.Copy, scale=-1.0 / P)
 
             for q in range(NU):
-                cols = slice(q * UC, (q + 1) * UC)
                 for t in range(T):
                     tp = pst.tile([P, UC], BF16, tag="tp")
-                    for j in range(UNIT):
-                        nc.tensor.transpose(
-                            tp[:, j * P : (j + 1) * P],
-                            Y[:, q * UNIT + j, t * P : (t + 1) * P],
-                            ident[:],
+                    transposes(tp, q * UNIT, UNIT, t)
+                    if t < SP:
+                        junk = jpool.tile([P, UC], BF16, tag="junk")
+                        nc.scalar.activation(
+                            out=junk[:],
+                            in_=tp[:],
+                            func=ACT.Square,
+                            bias=negm0[:, t : t + 1],
+                            accum_out=sq[:, t * NU + q : t * NU + q + 1],
                         )
-                    nc.vector.tensor_copy(out=XT[:, t, cols], in_=tp[:])
-                nc.tensor.matmul(out=pump_ps[:], lhsT=wf[:, 0:P], rhs=wf[:], start=True, stop=True)
-                if q > 0:
-                    nc.vector.bn_stats(out=st[:, q - 1, :], in_=XT[:, SP, (q - 1) * UC : q * UC])
+                    else:
+                        nc.vector.bn_stats(out=st[:, t - SP, q, :], in_=tp[:])
                 if q % SUMQ == SUMQ - 1:
                     blk = q // SUMQ
                     ng = SUMQ * UNIT
                     for t in range(SP):
-                        col = (blk * SP + t) * SUMN
+                        col = blk * SP + t
                         for j in range(ng):
                             nc.tensor.matmul(
-                                out=sx_ps[:, col : col + SUMN],
+                                out=sx_ps[:, col : col + 1],
                                 lhsT=Y[:, blk * ng + j, t * P : (t + 1) * P],
-                                rhs=ones[:, 0:SUMN],
+                                rhs=ones[:, 0:1],
                                 start=(j == 0),
                                 stop=(j == ng - 1),
                             )
-                if q % SPAN == SPAN - 1:
-                    v = q // SPAN
-                    for t in range(SP):
-                        junk = jpool.tile([P, SPAN * UC], BF16, tag="junk")
-                        nc.scalar.activation(
-                            out=junk[:],
-                            in_=XT[:, t, v * SPAN * UC : (v + 1) * SPAN * UC],
-                            func=ACT.Square,
-                            bias=negm0[:, t : t + 1],
-                            accum_out=sq[:, t * NS + v : t * NS + v + 1],
-                        )
                 if q == 2:
                     wt_ps = pss.tile([P, T, O], BF16, tag="setup")
                     for t in range(T):
@@ -161,8 +146,9 @@ def tile_simclr_pa_t_kernel(tc, y_lin, gamma, beta, W2, b2, out):
                                 w_sb[:, h, t * P : (t + 1) * P],
                                 ident[:],
                             )
-                    nc.vector.tensor_copy(out=wg[:], in_=wt_ps[:].rearrange("p t o -> p o t"))
-                if q == 3:
+                    nc.scalar.copy(out=wt_sb[:], in_=wt_ps[:])
+                    nc.gpsimd.tensor_copy(out=wg[:], in_=wt_sb[:].rearrange("p t o -> p o t"))
+                if q == 6:
                     gb_ps = pss.tile([P, P], BF16, tag="setup")
                     nc.tensor.transpose(gb_ps[:], gb[:], ident[:])
                     nc.scalar.copy(out=gbT[:], in_=gb_ps[:, 0 : 2 * T])
@@ -170,56 +156,60 @@ def tile_simclr_pa_t_kernel(tc, y_lin, gamma, beta, W2, b2, out):
                     nc.tensor.matmul(out=b2_ps[:], lhsT=ones[:], rhs=b2z[:], start=True, stop=True)
                     for h in range(2):
                         nc.scalar.copy(out=b2b[:, h, :], in_=b2_ps[:])
-            nc.vector.bn_stats(out=st[:, NU - 1, :], in_=XT[:, SP, (NU - 1) * UC : NU * UC])
-            nc.vector.bn_aggr(out=mv[:, SP, :], in_=st[:].rearrange("p q s -> p (q s)"))
+
             nc.vector.tensor_reduce(
-                out=sxs[:],
-                in_=sx_ps[:].rearrange("p (k t n) -> p t k n", t=SP, n=SUMN)[:, :, :, 0],
-                axis=AX.X,
-                op=ALU.add,
+                out=sxs[:], in_=sx_ps[:].rearrange("p (k t) -> p t k", t=SP), axis=AX.X, op=ALU.add
             )
+            nc.vector.bn_aggr(out=mv[:, SP, :], in_=st[:, 0].rearrange("p q s -> p (q s)"))
             nc.vector.scalar_tensor_tensor(
                 out=dm[:], in0=sxs[:], scalar=1.0 / B, in1=negm0[:], op0=ALU.mult, op1=ALU.add
             )
+            nc.vector.bn_aggr(out=mv[:, SP + 1, :], in_=st[:, 1].rearrange("p q s -> p (q s)"))
             nc.vector.tensor_tensor(out=dm2[:], in0=dm[:], in1=dm[:], op=ALU.mult)
+            nc.vector.tensor_reduce(
+                out=sqs[:], in_=sq[:].rearrange("p (t q) -> p t q", q=NU), axis=AX.X, op=ALU.add
+            )
             nc.vector.tensor_tensor(out=mv[:, 0:SP, 0], in0=dm[:], in1=negm0[:], op=ALU.subtract)
+            nc.vector.scalar_tensor_tensor(
+                out=mv[:, 0:SP, 1], in0=sqs[:], scalar=1.0 / B, in1=dm2[:], op0=ALU.mult, op1=ALU.subtract
+            )
+            nc.scalar.activation(out=std[:], in_=mv[:, :, 1], func=ACT.Sqrt, bias=eps[:, 0:1])
+            nc.vector.scalar_tensor_tensor(
+                out=nmg[:], in0=mv[:, :, 0], scalar=-1.0, in1=gbT[:, 0:T], op0=ALU.mult, op1=ALU.mult
+            )
             nc.vector.quantize_mx(
                 out=w_codes[:].bitcast(FP8X4),
                 scales=w_scales[:],
                 in_=wg[:].rearrange("p o t -> p (o t)"),
             )
-            nc.vector.tensor_reduce(
-                out=sqs[:], in_=sq[:].rearrange("p (t v) -> p t v", v=NS), axis=AX.X, op=ALU.add
-            )
-            nc.vector.scalar_tensor_tensor(
-                out=mv[:, 0:SP, 1], in0=sqs[:], scalar=1.0 / B, in1=dm2[:], op0=ALU.mult, op1=ALU.subtract
-            )
-            nc.scalar.activation(out=std[:], in_=mv[:, :, 1], func=ACT.Sqrt, bias=eps[:, 0:1])
             nc.vector.reciprocal(out=rstd[:], in_=std[:])
-            nc.vector.tensor_tensor(out=sc[:], in0=gbT[:, 0:T], in1=rstd[:], op=ALU.mult)
-            nc.vector.tensor_tensor(out=ms[:], in0=mv[:, :, 0], in1=sc[:], op=ALU.mult)
-            nc.vector.tensor_tensor(out=sh[:], in0=gbT[:, T : 2 * T], in1=ms[:], op=ALU.subtract)
 
         zpool = ctx.enter_context(tc.tile_pool(name="zpool", bufs=2))
         gpool = ctx.enter_context(tc.tile_pool(name="gpool", bufs=3))
         qpool = ctx.enter_context(tc.tile_pool(name="qpool", bufs=3))
-        ppool = ctx.enter_context(tc.tile_pool(name="ppool", bufs=4))
-        spool = ctx.enter_context(tc.tile_pool(name="spool", bufs=4))
+        ppool = ctx.enter_context(tc.tile_pool(name="ppool", bufs=5))
+        spool = ctx.enter_context(tc.tile_pool(name="spool", bufs=5))
         kpool = ctx.enter_context(tc.tile_pool(name="kpool", bufs=2))
-        psm = ctx.enter_context(tc.psum_pool(name="psm", bufs=8))
-        CMAX = max(CHUNKS)
+        ptq = ctx.enter_context(tc.psum_pool(name="ptq", bufs=T))
+        psm = ctx.enter_context(tc.psum_pool(name="psm", bufs=CMAX // 2))
         NCH = len(CHUNKS)
         starts = [sum(CHUNKS[:c]) for c in range(NCH)]
-        Zs, Gs, Cs, Ss, As, Ps, SSs, RIs = {}, {}, {}, {}, {}, {}, {}, {}
+        Xs, Zs, Gs, Cs, Ss, As, Ps, Ns, RIs = {}, {}, {}, {}, {}, {}, {}, {}, {}
+
+        def transpose_chunk(c):
+            Xs[c] = []
+            for t in range(T):
+                tq = ptq.tile([P, CMAX * P], BF16, tag="tq", name="tq")
+                transposes(tq, starts[c], CHUNKS[c], t)
+                Xs[c].append(tq)
 
         def affine(c):
             n = CHUNKS[c] * P
-            c0 = starts[c] * P
             Zs[c] = zpool.tile([P, T, CMAX * P], BF16, tag="Z", name="Z")
             for t in range(T):
                 nc.vector.tensor_scalar(
                     out=Zs[c][:, t, 0:n],
-                    in0=XT[:, t, c0 : c0 + n],
+                    in0=Xs[c][t][:, 0:n],
                     scalar1=sc[:, t : t + 1],
                     scalar2=sh[:, t : t + 1],
                     op0=ALU.mult,
@@ -228,7 +218,7 @@ def tile_simclr_pa_t_kernel(tc, y_lin, gamma, beta, W2, b2, out):
 
         def regroup(c):
             n = CHUNKS[c] * P
-            cv = n - (n // 2 if c < 2 else 3 * n // 8)
+            cv = 3 * n // 8
             Gs[c] = gpool.tile([P, CMAX * P, T], BF16, tag="Gt", name="Gt", align_bytes=64)
             nc.vector.tensor_scalar(
                 out=Gs[c][:, 0:cv, :].rearrange("p (c i) t -> p c t i", i=4),
@@ -237,12 +227,11 @@ def tile_simclr_pa_t_kernel(tc, y_lin, gamma, beta, W2, b2, out):
                 scalar2=None,
                 op0=ALU.max,
             )
-            if cv < n:
-                nc.scalar.activation(
-                    out=Gs[c][:, cv:n, :].rearrange("p (c i) t -> p c t i", i=4),
-                    in_=Zs[c][:, :, cv:n].rearrange("p t (c i) -> p c t i", i=4),
-                    func=ACT.Relu,
-                )
+            nc.scalar.activation(
+                out=Gs[c][:, cv:n, :].rearrange("p (c i) t -> p c t i", i=4),
+                in_=Zs[c][:, :, cv:n].rearrange("p t (c i) -> p c t i", i=4),
+                func=ACT.Relu,
+            )
 
         def quantise_multiply(c):
             n = CHUNKS[c] * P
@@ -272,7 +261,8 @@ def tile_simclr_pa_t_kernel(tc, y_lin, gamma, beta, W2, b2, out):
         def bias_squares(c):
             ng = CHUNKS[c]
             Ps[c] = ppool.tile([P, CMAX, O], F32, tag="Pt", name="Pt")
-            SSs[c] = spool.tile([P, CMAX], F32, tag="ss", name="ss")
+            ss = spool.tile([P, CMAX], F32, tag="ss")
+            Ns[c] = spool.tile([P, CMAX], F32, tag="nrm", name="nrm")
             for i in range(ng // 2):
                 nc.vector.tensor_tensor(
                     out=Ps[c][:, 2 * i : 2 * i + 2, :], in0=As[c][i][:], in1=b2b[:], op=ALU.add
@@ -280,25 +270,27 @@ def tile_simclr_pa_t_kernel(tc, y_lin, gamma, beta, W2, b2, out):
             for r in range(ng):
                 junk2 = kpool.tile([P, O], BF16, tag="junk2")
                 nc.scalar.activation(
-                    out=junk2[:], in_=Ps[c][:, r, :], func=ACT.Square, accum_out=SSs[c][:, r : r + 1]
+                    out=junk2[:], in_=Ps[c][:, r, :], func=ACT.Square, accum_out=ss[:, r : r + 1]
                 )
-            nrm = spool.tile([P, CMAX], F32, tag="nrm")
-            nc.scalar.activation(out=nrm[:, 0:ng], in_=SSs[c][:, 0:ng], func=ACT.Sqrt, bias=tiny[:, 0:1])
-            SSs[c] = nrm
+            nc.scalar.activation(out=Ns[c][:, 0:ng], in_=ss[:, 0:ng], func=ACT.Sqrt, bias=tiny[:, 0:1])
 
-        def inverse_norm(c):
+        def clamp_norm(c):
             ng = CHUNKS[c]
-            nrc = spool.tile([P, CMAX], F32, tag="nrc")
-            RIs[c] = spool.tile([P, CMAX], F32, tag="rinv", name="rinv")
+            nrc = spool.tile([P, CMAX], F32, tag="nrc", name="nrc")
             nc.vector.tensor_scalar(
-                out=nrc[:, 0:ng], in0=SSs[c][:, 0:ng], scalar1=L2_EPS, scalar2=None, op0=ALU.max
+                out=nrc[:, 0:ng], in0=Ns[c][:, 0:ng], scalar1=L2_EPS, scalar2=None, op0=ALU.max
             )
-            nc.vector.reciprocal(out=RIs[c][:, 0:ng], in_=nrc[:, 0:ng])
+            Ns[c] = nrc
+
+        def invert_norm(c):
+            ng = CHUNKS[c]
+            RIs[c] = spool.tile([P, CMAX], F32, tag="rinv", name="rinv")
+            nc.vector.reciprocal(out=RIs[c][:, 0:ng], in_=Ns[c][:, 0:ng])
 
         def scale_store(c):
             ng = CHUNKS[c]
             for r in range(ng):
-                if r < V_SCALE:
+                if r < 3 * ng // 4:
                     nc.vector.tensor_scalar(
                         out=Ps[c][:, r, :],
                         in0=Ps[c][:, r, :],
@@ -312,17 +304,33 @@ def tile_simclr_pa_t_kernel(tc, y_lin, gamma, beta, W2, b2, out):
                     )
             nc.sync.dma_start(out=ov[:, starts[c] : starts[c] + ng, :], in_=Ps[c][:, 0:ng, :])
 
+        transpose_chunk(0)
+        nc.vector.tensor_tensor(out=sc[:], in0=gbT[:, 0:T], in1=rstd[:], op=ALU.mult)
+        for t in range(T):
+            nc.vector.tensor_scalar(
+                out=sh[:, t : t + 1],
+                in0=rstd[:, t : t + 1],
+                scalar1=nmg[:, t : t + 1],
+                scalar2=gbT[:, T + t : T + t + 1],
+                op0=ALU.mult,
+                op1=ALU.add,
+            )
         affine(0)
+        transpose_chunk(1)
         for i in range(NCH + 2):
-            if 0 <= i - 2:
-                inverse_norm(i - 2)
             if i < NCH:
                 regroup(i)
             if 0 <= i - 2:
-                scale_store(i - 2)
+                clamp_norm(i - 2)
             if i + 1 < NCH:
                 affine(i + 1)
+            if i + 2 < NCH:
+                transpose_chunk(i + 2)
+            if 0 <= i - 2:
+                invert_norm(i - 2)
             if 0 <= i - 1 < NCH:
                 bias_squares(i - 1)
+            if 0 <= i - 2:
+                scale_store(i - 2)
             if i < NCH:
                 quantise_multiply(i)

@@ -28,7 +28,7 @@ SUMQ = 4
 BN_EPS = 1e-5
 L2_EPS = 1e-12
 LOAD_BOUNDS = [0, 4, 8, 16, 24, 32, 40, 48, 56, 64]
-CHUNKS = [8, 8, 8, 8, 8, 8, 8, 4, 4]
+CHUNKS = [8, 8, 8, 8, 8, 8, 8, 4, 2, 2]
 CMAX = 8
 
 
@@ -289,8 +289,18 @@ def tile_simclr_pa_t_kernel(tc, y_lin, gamma, beta, W2, b2, out):
 
         def scale_store(c):
             ng = CHUNKS[c]
+            last = c >= NCH - 2
             for r in range(ng):
-                if r < 3 * ng // 4:
+                if r < ng // 2 and not last:
+                    nc.gpsimd.tensor_scalar(
+                        out=Ps[c][:, r, :],
+                        in0=Ps[c][:, r, :],
+                        scalar1=RIs[c][:, r : r + 1],
+                        scalar2=1.0,
+                        op0=ALU.mult,
+                        op1=ALU.mult,
+                    )
+                elif r < 3 * ng // 4 or last:
                     nc.vector.tensor_scalar(
                         out=Ps[c][:, r, :],
                         in0=Ps[c][:, r, :],

@@ -203,22 +203,33 @@ def tile_simclr_pa_t_kernel(tc, y_lin, gamma, beta, W2, b2, out):
                 transposes(tq, starts[c], CHUNKS[c], t)
                 Xs[c].append(tq)
 
-        def affine(c):
+        def affine(c, after_first_plane=None):
             n = CHUNKS[c] * P
             Zs[c] = zpool.tile([P, T, CMAX * P], BF16, tag="Z", name="Z")
             for t in range(T):
-                nc.vector.tensor_scalar(
-                    out=Zs[c][:, t, 0:n],
-                    in0=Xs[c][t][:, 0:n],
-                    scalar1=sc[:, t : t + 1],
-                    scalar2=sh[:, t : t + 1],
-                    op0=ALU.mult,
-                    op1=ALU.add,
-                )
+                if c < 2 and t >= 2:
+                    nc.scalar.activation(
+                        out=Zs[c][:, t, 0:n],
+                        in_=Xs[c][t][:, 0:n],
+                        func=ACT.Identity,
+                        scale=sc[:, t : t + 1],
+                        bias=sh[:, t : t + 1],
+                    )
+                else:
+                    nc.vector.tensor_scalar(
+                        out=Zs[c][:, t, 0:n],
+                        in0=Xs[c][t][:, 0:n],
+                        scalar1=sc[:, t : t + 1],
+                        scalar2=sh[:, t : t + 1],
+                        op0=ALU.mult,
+                        op1=ALU.add,
+                    )
+                if t == 0 and after_first_plane is not None:
+                    invert_norm(after_first_plane)
 
         def regroup(c):
             n = CHUNKS[c] * P
-            cv = 3 * n // 8
+            cv = 5 * n // 16
             Gs[c] = gpool.tile([P, CMAX * P, T], BF16, tag="Gt", name="Gt", align_bytes=64)
             nc.vector.tensor_scalar(
                 out=Gs[c][:, 0:cv, :].rearrange("p (c i) t -> p c t i", i=4),
@@ -290,27 +301,24 @@ def tile_simclr_pa_t_kernel(tc, y_lin, gamma, beta, W2, b2, out):
         def scale_store(c):
             ng = CHUNKS[c]
             last = c >= NCH - 2
+            rinv = RIs[c]
             for r in range(ng):
-                if r < ng // 2 and not last:
+                if r < 3 * ng // 4 and not last:
                     nc.gpsimd.tensor_scalar(
                         out=Ps[c][:, r, :],
                         in0=Ps[c][:, r, :],
-                        scalar1=RIs[c][:, r : r + 1],
+                        scalar1=rinv[:, r : r + 1],
                         scalar2=1.0,
                         op0=ALU.mult,
                         op1=ALU.mult,
                     )
-                elif r < 3 * ng // 4 or last:
+                else:
                     nc.vector.tensor_scalar(
                         out=Ps[c][:, r, :],
                         in0=Ps[c][:, r, :],
-                        scalar1=RIs[c][:, r : r + 1],
+                        scalar1=rinv[:, r : r + 1],
                         scalar2=None,
                         op0=ALU.mult,
-                    )
-                else:
-                    nc.scalar.activation(
-                        out=Ps[c][:, r, :], in_=Ps[c][:, r, :], func=ACT.Copy, scale=RIs[c][:, r : r + 1]
                     )
             nc.sync.dma_start(out=ov[:, starts[c] : starts[c] + ng, :], in_=Ps[c][:, 0:ng, :])
 
@@ -327,20 +335,21 @@ def tile_simclr_pa_t_kernel(tc, y_lin, gamma, beta, W2, b2, out):
             )
         affine(0)
         transpose_chunk(1)
+        regroup(0)
         for i in range(NCH + 2):
-            if i < NCH:
-                regroup(i)
             if 0 <= i - 2:
                 clamp_norm(i - 2)
             if i + 1 < NCH:
-                affine(i + 1)
+                affine(i + 1, after_first_plane=(i - 2 if i >= 2 else None))
+            elif 0 <= i - 2:
+                invert_norm(i - 2)
             if i + 2 < NCH:
                 transpose_chunk(i + 2)
-            if 0 <= i - 2:
-                invert_norm(i - 2)
             if 0 <= i - 1 < NCH:
                 bias_squares(i - 1)
             if 0 <= i - 2:
                 scale_store(i - 2)
             if i < NCH:
                 quantise_multiply(i)
+            if i + 1 < NCH:
+                regroup(i + 1)

@@ -146,16 +146,16 @@ def tile_simclr_pa_t_kernel(tc, y_lin, gamma, beta, W2, b2, out):
                                 w_sb[:, h, t * P : (t + 1) * P],
                                 ident[:],
                             )
-                    nc.scalar.copy(out=wt_sb[:], in_=wt_ps[:])
+                    nc.vector.tensor_copy(out=wt_sb[:], in_=wt_ps[:])
                     nc.gpsimd.tensor_copy(out=wg[:], in_=wt_sb[:].rearrange("p t o -> p o t"))
                 if q == 6:
                     gb_ps = pss.tile([P, P], BF16, tag="setup")
                     nc.tensor.transpose(gb_ps[:], gb[:], ident[:])
-                    nc.scalar.copy(out=gbT[:], in_=gb_ps[:, 0 : 2 * T])
+                    nc.vector.tensor_copy(out=gbT[:], in_=gb_ps[:, 0 : 2 * T])
                     b2_ps = pss.tile([P, O], F32, tag="setup")
                     nc.tensor.matmul(out=b2_ps[:], lhsT=ones[:], rhs=b2z[:], start=True, stop=True)
                     for h in range(2):
-                        nc.scalar.copy(out=b2b[:, h, :], in_=b2_ps[:])
+                        nc.vector.tensor_copy(out=b2b[:, h, :], in_=b2_ps[:])
 
             nc.vector.tensor_reduce(
                 out=sxs[:], in_=sx_ps[:].rearrange("p (k t) -> p t k", t=SP), axis=AX.X, op=ALU.add
@@ -203,7 +203,7 @@ def tile_simclr_pa_t_kernel(tc, y_lin, gamma, beta, W2, b2, out):
                 transposes(tq, starts[c], CHUNKS[c], t)
                 Xs[c].append(tq)
 
-        def affine(c, after_first_plane=None):
+        def affine(c):
             n = CHUNKS[c] * P
             Zs[c] = zpool.tile([P, T, CMAX * P], BF16, tag="Z", name="Z")
             for t in range(T):
@@ -224,12 +224,10 @@ def tile_simclr_pa_t_kernel(tc, y_lin, gamma, beta, W2, b2, out):
                         op0=ALU.mult,
                         op1=ALU.add,
                     )
-                if t == 0 and after_first_plane is not None:
-                    invert_norm(after_first_plane)
 
         def regroup(c):
             n = CHUNKS[c] * P
-            cv = 5 * n // 16
+            cv = 3 * n // 8
             Gs[c] = gpool.tile([P, CMAX * P, T], BF16, tag="Gt", name="Gt", align_bytes=64)
             nc.vector.tensor_scalar(
                 out=Gs[c][:, 0:cv, :].rearrange("p (c i) t -> p c t i", i=4),
@@ -301,24 +299,27 @@ def tile_simclr_pa_t_kernel(tc, y_lin, gamma, beta, W2, b2, out):
         def scale_store(c):
             ng = CHUNKS[c]
             last = c >= NCH - 2
-            rinv = RIs[c]
             for r in range(ng):
-                if r < 3 * ng // 4 and not last:
+                if r < ng // 2 and not last:
                     nc.gpsimd.tensor_scalar(
                         out=Ps[c][:, r, :],
                         in0=Ps[c][:, r, :],
-                        scalar1=rinv[:, r : r + 1],
+                        scalar1=RIs[c][:, r : r + 1],
                         scalar2=1.0,
                         op0=ALU.mult,
                         op1=ALU.mult,
                     )
-                else:
+                elif r < 3 * ng // 4 or last:
                     nc.vector.tensor_scalar(
                         out=Ps[c][:, r, :],
                         in0=Ps[c][:, r, :],
-                        scalar1=rinv[:, r : r + 1],
+                        scalar1=RIs[c][:, r : r + 1],
                         scalar2=None,
                         op0=ALU.mult,
+                    )
+                else:
+                    nc.scalar.activation(
+                        out=Ps[c][:, r, :], in_=Ps[c][:, r, :], func=ACT.Copy, scale=RIs[c][:, r : r + 1]
                     )
             nc.sync.dma_start(out=ov[:, starts[c] : starts[c] + ng, :], in_=Ps[c][:, 0:ng, :])
 
@@ -335,21 +336,20 @@ def tile_simclr_pa_t_kernel(tc, y_lin, gamma, beta, W2, b2, out):
             )
         affine(0)
         transpose_chunk(1)
-        regroup(0)
         for i in range(NCH + 2):
+            if i < NCH:
+                regroup(i)
             if 0 <= i - 2:
                 clamp_norm(i - 2)
             if i + 1 < NCH:
-                affine(i + 1, after_first_plane=(i - 2 if i >= 2 else None))
-            elif 0 <= i - 2:
-                invert_norm(i - 2)
+                affine(i + 1)
             if i + 2 < NCH:
                 transpose_chunk(i + 2)
+            if 0 <= i - 2:
+                invert_norm(i - 2)
             if 0 <= i - 1 < NCH:
                 bias_squares(i - 1)
             if 0 <= i - 2:
                 scale_store(i - 2)
             if i < NCH:
                 quantise_multiply(i)
-            if i + 1 < NCH:
-                regroup(i + 1)

@@ -146,16 +146,16 @@ def tile_simclr_pa_t_kernel(tc, y_lin, gamma, beta, W2, b2, out):
                                 w_sb[:, h, t * P : (t + 1) * P],
                                 ident[:],
                             )
-                    nc.vector.tensor_copy(out=wt_sb[:], in_=wt_ps[:])
+                    nc.scalar.copy(out=wt_sb[:], in_=wt_ps[:])
                     nc.gpsimd.tensor_copy(out=wg[:], in_=wt_sb[:].rearrange("p t o -> p o t"))
                 if q == 6:
                     gb_ps = pss.tile([P, P], BF16, tag="setup")
                     nc.tensor.transpose(gb_ps[:], gb[:], ident[:])
-                    nc.vector.tensor_copy(out=gbT[:], in_=gb_ps[:, 0 : 2 * T])
+                    nc.scalar.copy(out=gbT[:], in_=gb_ps[:, 0 : 2 * T])
                     b2_ps = pss.tile([P, O], F32, tag="setup")
                     nc.tensor.matmul(out=b2_ps[:], lhsT=ones[:], rhs=b2z[:], start=True, stop=True)
                     for h in range(2):
-                        nc.vector.tensor_copy(out=b2b[:, h, :], in_=b2_ps[:])
+                        nc.scalar.copy(out=b2b[:, h, :], in_=b2_ps[:])
 
             nc.vector.tensor_reduce(
                 out=sxs[:], in_=sx_ps[:].rearrange("p (k t) -> p t k", t=SP), axis=AX.X, op=ALU.add
@@ -194,73 +194,64 @@ def tile_simclr_pa_t_kernel(tc, y_lin, gamma, beta, W2, b2, out):
         psm = ctx.enter_context(tc.psum_pool(name="psm", bufs=CMAX // 2))
         NCH = len(CHUNKS)
         starts = [sum(CHUNKS[:c]) for c in range(NCH)]
-        Xs, Zs, Gs, Cs, Ss, As, Ps, Ns, RIs = {}, {}, {}, {}, {}, {}, {}, {}, {}
+        planes, shifted, grouped, codes, scales, sums, rows, norms, inverse = {}, {}, {}, {}, {}, {}, {}, {}, {}
 
         def transpose_chunk(c):
-            Xs[c] = []
+            planes[c] = []
             for t in range(T):
                 tq = ptq.tile([P, CMAX * P], BF16, tag="tq", name="tq")
                 transposes(tq, starts[c], CHUNKS[c], t)
-                Xs[c].append(tq)
+                planes[c].append(tq)
 
         def affine(c):
-            n = CHUNKS[c] * P
-            Zs[c] = zpool.tile([P, T, CMAX * P], BF16, tag="Z", name="Z")
+            width = CHUNKS[c] * P
+            shifted[c] = zpool.tile([P, T, CMAX * P], BF16, tag="Z", name="Z")
             for t in range(T):
-                if c < 2 and t >= 2:
-                    nc.scalar.activation(
-                        out=Zs[c][:, t, 0:n],
-                        in_=Xs[c][t][:, 0:n],
-                        func=ACT.Identity,
-                        scale=sc[:, t : t + 1],
-                        bias=sh[:, t : t + 1],
-                    )
-                else:
-                    nc.vector.tensor_scalar(
-                        out=Zs[c][:, t, 0:n],
-                        in0=Xs[c][t][:, 0:n],
-                        scalar1=sc[:, t : t + 1],
-                        scalar2=sh[:, t : t + 1],
-                        op0=ALU.mult,
-                        op1=ALU.add,
-                    )
+                nc.vector.tensor_scalar(
+                    out=shifted[c][:, t, 0:width],
+                    in0=planes[c][t][:, 0:width],
+                    scalar1=sc[:, t : t + 1],
+                    scalar2=sh[:, t : t + 1],
+                    op0=ALU.mult,
+                    op1=ALU.add,
+                )
 
         def regroup(c):
-            n = CHUNKS[c] * P
-            cv = 3 * n // 8
-            Gs[c] = gpool.tile([P, CMAX * P, T], BF16, tag="Gt", name="Gt", align_bytes=64)
+            width = CHUNKS[c] * P
+            split = width // 4
+            grouped[c] = gpool.tile([P, CMAX * P, T], BF16, tag="Gt", name="Gt", align_bytes=64)
             nc.vector.tensor_scalar(
-                out=Gs[c][:, 0:cv, :].rearrange("p (c i) t -> p c t i", i=4),
-                in0=Zs[c][:, :, 0:cv].rearrange("p t (c i) -> p c t i", i=4),
+                out=grouped[c][:, 0:split, :].rearrange("p (c i) t -> p c t i", i=4),
+                in0=shifted[c][:, :, 0:split].rearrange("p t (c i) -> p c t i", i=4),
                 scalar1=0.0,
                 scalar2=None,
                 op0=ALU.max,
             )
             nc.scalar.activation(
-                out=Gs[c][:, cv:n, :].rearrange("p (c i) t -> p c t i", i=4),
-                in_=Zs[c][:, :, cv:n].rearrange("p t (c i) -> p c t i", i=4),
+                out=grouped[c][:, split:width, :].rearrange("p (c i) t -> p c t i", i=4),
+                in_=shifted[c][:, :, split:width].rearrange("p t (c i) -> p c t i", i=4),
                 func=ACT.Relu,
             )
 
         def quantise_multiply(c):
-            n = CHUNKS[c] * P
-            Cs[c] = qpool.tile([P, CMAX * P], U32, tag="codes", name="codes", align_bytes=64)
-            Ss[c] = qpool.tile([P, CMAX * P], U8, tag="scales", name="scales", align_bytes=64)
+            width = CHUNKS[c] * P
+            codes[c] = qpool.tile([P, CMAX * P], U32, tag="codes", name="codes", align_bytes=64)
+            scales[c] = qpool.tile([P, CMAX * P], U8, tag="scales", name="scales", align_bytes=64)
             nc.vector.quantize_mx(
-                out=Cs[c][:, 0:n].bitcast(FP8X4),
-                scales=Ss[c][:, 0:n],
-                in_=Gs[c][:, 0:n, :].rearrange("p b t -> p (b t)"),
+                out=codes[c][:, 0:width].bitcast(FP8X4),
+                scales=scales[c][:, 0:width],
+                in_=grouped[c][:, 0:width, :].rearrange("p b t -> p (b t)"),
             )
-            As[c] = []
+            sums[c] = []
             for i in range(CHUNKS[c] // 2):
                 acc = psm.tile([P, 2, O], F32, tag="acc", name="acc")
-                As[c].append(acc)
+                sums[c].append(acc)
                 for h in range(2):
                     m = slice((2 * i + h) * P, (2 * i + h + 1) * P)
                     nc.tensor.matmul_mx(
                         out=acc[:, h, :],
-                        lhsT=Cs[c][:, m].bitcast(FP8X4),
-                        lhsT_scale=Ss[c][:, m],
+                        lhsT=codes[c][:, m].bitcast(FP8X4),
+                        lhsT_scale=scales[c][:, m],
                         rhs=w_codes[:].bitcast(FP8X4),
                         rhs_scale=w_scales[:],
                         start=True,
@@ -268,60 +259,56 @@ def tile_simclr_pa_t_kernel(tc, y_lin, gamma, beta, W2, b2, out):
                     )
 
         def bias_squares(c):
-            ng = CHUNKS[c]
-            Ps[c] = ppool.tile([P, CMAX, O], F32, tag="Pt", name="Pt")
+            tiles = CHUNKS[c]
+            rows[c] = ppool.tile([P, CMAX, O], F32, tag="Pt", name="Pt")
             ss = spool.tile([P, CMAX], F32, tag="ss")
-            Ns[c] = spool.tile([P, CMAX], F32, tag="nrm", name="nrm")
-            for i in range(ng // 2):
+            norms[c] = spool.tile([P, CMAX], F32, tag="nrm", name="nrm")
+            for i in range(tiles // 2):
                 nc.vector.tensor_tensor(
-                    out=Ps[c][:, 2 * i : 2 * i + 2, :], in0=As[c][i][:], in1=b2b[:], op=ALU.add
+                    out=rows[c][:, 2 * i : 2 * i + 2, :], in0=sums[c][i][:], in1=b2b[:], op=ALU.add
                 )
-            for r in range(ng):
+            for r in range(tiles):
                 junk2 = kpool.tile([P, O], BF16, tag="junk2")
                 nc.scalar.activation(
-                    out=junk2[:], in_=Ps[c][:, r, :], func=ACT.Square, accum_out=ss[:, r : r + 1]
+                    out=junk2[:], in_=rows[c][:, r, :], func=ACT.Square, accum_out=ss[:, r : r + 1]
                 )
-            nc.scalar.activation(out=Ns[c][:, 0:ng], in_=ss[:, 0:ng], func=ACT.Sqrt, bias=tiny[:, 0:1])
+            nc.scalar.activation(out=norms[c][:, 0:tiles], in_=ss[:, 0:tiles], func=ACT.Sqrt, bias=tiny[:, 0:1])
 
         def clamp_norm(c):
-            ng = CHUNKS[c]
+            tiles = CHUNKS[c]
             nrc = spool.tile([P, CMAX], F32, tag="nrc", name="nrc")
             nc.vector.tensor_scalar(
-                out=nrc[:, 0:ng], in0=Ns[c][:, 0:ng], scalar1=L2_EPS, scalar2=None, op0=ALU.max
+                out=nrc[:, 0:tiles], in0=norms[c][:, 0:tiles], scalar1=L2_EPS, scalar2=None, op0=ALU.max
             )
-            Ns[c] = nrc
+            norms[c] = nrc
 
         def invert_norm(c):
-            ng = CHUNKS[c]
-            RIs[c] = spool.tile([P, CMAX], F32, tag="rinv", name="rinv")
-            nc.vector.reciprocal(out=RIs[c][:, 0:ng], in_=Ns[c][:, 0:ng])
+            tiles = CHUNKS[c]
+            inverse[c] = spool.tile([P, CMAX], F32, tag="rinv", name="rinv")
+            nc.vector.reciprocal(out=inverse[c][:, 0:tiles], in_=norms[c][:, 0:tiles])
 
         def scale_store(c):
-            ng = CHUNKS[c]
-            last = c >= NCH - 2
-            for r in range(ng):
-                if r < ng // 2 and not last:
+            tiles = CHUNKS[c]
+            vector_only = c >= NCH - 2
+            for r in range(tiles):
+                if r < tiles // 2 and not vector_only:
                     nc.gpsimd.tensor_scalar(
-                        out=Ps[c][:, r, :],
-                        in0=Ps[c][:, r, :],
-                        scalar1=RIs[c][:, r : r + 1],
+                        out=rows[c][:, r, :],
+                        in0=rows[c][:, r, :],
+                        scalar1=inverse[c][:, r : r + 1],
                         scalar2=1.0,
                         op0=ALU.mult,
                         op1=ALU.mult,
                     )
-                elif r < 3 * ng // 4 or last:
+                else:
                     nc.vector.tensor_scalar(
-                        out=Ps[c][:, r, :],
-                        in0=Ps[c][:, r, :],
-                        scalar1=RIs[c][:, r : r + 1],
+                        out=rows[c][:, r, :],
+                        in0=rows[c][:, r, :],
+                        scalar1=inverse[c][:, r : r + 1],
                         scalar2=None,
                         op0=ALU.mult,
                     )
-                else:
-                    nc.scalar.activation(
-                        out=Ps[c][:, r, :], in_=Ps[c][:, r, :], func=ACT.Copy, scale=RIs[c][:, r : r + 1]
-                    )
-            nc.sync.dma_start(out=ov[:, starts[c] : starts[c] + ng, :], in_=Ps[c][:, 0:ng, :])
+            nc.sync.dma_start(out=ov[:, starts[c] : starts[c] + tiles, :], in_=rows[c][:, 0:tiles, :])
 
         transpose_chunk(0)
         nc.vector.tensor_tensor(out=sc[:], in0=gbT[:, 0:T], in1=rstd[:], op=ALU.mult)

from contextlib import ExitStack

import concourse.mybir as mybir
from concourse.masks import make_identity

FLOPS = 2 * 8192 * 512 * 256

FP8X4 = mybir.dt.float8_e4m3fn_x4
BF16 = mybir.dt.bfloat16
F32 = mybir.dt.float32
U32 = mybir.dt.uint32
U8 = mybir.dt.uint8
ALU = mybir.AluOpType
ACT = mybir.ActivationFunctionType
AX = mybir.AxisListType

P = 128
B = 8192
K = 512
O = 256
T = K // P
G = B // P
UNIT = 4
NU = G // UNIT
UC = UNIT * P
SP = 2
SUMQ = 4
BN_EPS = 1e-5
L2_EPS = 1e-12
LOAD_BOUNDS = [0, 4, 8, 16, 24, 32, 40, 48, 56, 64]
CHUNKS = [8, 8, 8, 8, 8, 8, 8, 4, 2, 2]
CMAX = 8


def tile_simclr_pa_t_kernel(tc, y_lin, gamma, beta, W2, b2, out):
    nc = tc.nc
    yv = y_lin.rearrange("(p g) k -> p g k", g=G)
    ov = out.rearrange("(p g) o -> p g o", g=G)
    with ExitStack() as ctx:
        ctx.enter_context(tc.manual_schedule())
        const = ctx.enter_context(tc.tile_pool(name="const", bufs=1))
        Y = const.tile([P, G, K], BF16, name="Y")
        one1 = const.tile([P, 1], F32, name="one1")
        warm = const.tile([P, 1], F32, name="warm")
        eps = const.tile([P, 1], F32, name="eps")
        tiny = const.tile([P, 1], F32, name="tiny")
        ident = const.tile([P, P], BF16, name="ident")
        ones = const.tile([P, P], BF16, name="ones")
        gb = const.tile([P, P], BF16, name="gb")
        gbT = const.tile([P, 2 * T], F32, name="gbT")
        b2z = const.tile([P, O], BF16, name="b2z")
        b2b = const.tile([P, 2, O], F32, name="b2b")
        w_sb = const.tile([P, 2, K], BF16, name="w_sb")
        wt_sb = const.tile([P, T, O], BF16, name="wt_sb")
        wg = const.tile([P, O, T], BF16, name="wg", align_bytes=64)
        w_codes = const.tile([P, O], U32, name="w_codes", align_bytes=64)
        w_scales = const.tile([P, O], U8, name="w_scales", align_bytes=64)
        negm0 = const.tile([P, SP], F32, name="negm0")
        sq = const.tile([P, SP * NU], F32, name="sq")
        st = const.tile([P, T - SP, NU, 6], F32, name="st")
        mv = const.tile([P, T, 2], F32, name="mv")
        sxs = const.tile([P, SP], F32, name="sxs")
        sqs = const.tile([P, SP], F32, name="sqs")
        dm = const.tile([P, SP], F32, name="dm")
        dm2 = const.tile([P, SP], F32, name="dm2")
        nmg = const.tile([P, T], F32, name="nmg")
        std = const.tile([P, T], F32, name="std")
        rstd = const.tile([P, T], F32, name="rstd")
        sc = const.tile([P, T], F32, name="sc")
        sh = const.tile([P, T], F32, name="sh")

        nc.vector.memset(gb[:], 0.0)
        nc.vector.memset(b2z[:], 0.0)
        nc.scalar.dma_start(out=gb[0:T, :], in_=gamma.rearrange("(t p) -> t p", p=P))
        nc.scalar.dma_start(out=gb[T : 2 * T, :], in_=beta.rearrange("(t p) -> t p", p=P))
        nc.scalar.dma_start(out=b2z[0:1, :], in_=b2.rearrange("(a o) -> a o", a=1))
        for i in range(len(LOAD_BOUNDS) - 1):
            g0, g1 = LOAD_BOUNDS[i], LOAD_BOUNDS[i + 1]
            nc.sync.dma_start(out=Y[:, g0:g1, :], in_=yv[:, g0:g1, :])
            if i == 1:
                nc.sync.dma_start(out=w_sb[:], in_=W2.rearrange("(h o) k -> o h k", o=P))
        nc.vector.memset(one1[:], 1.0)
        nc.scalar.activation(out=warm[:], in_=one1[:], func=ACT.Sqrt)
        nc.vector.memset(ones[:], 1.0)
        nc.vector.memset(eps[:], BN_EPS)
        nc.vector.memset(tiny[:], 1e-30)
        make_identity(nc, ident[:])

        def transposes(dst, g0, n, t):
            for j in range(n):
                nc.tensor.transpose(
                    dst[:, j * P : (j + 1) * P], Y[:, g0 + j, t * P : (t + 1) * P], ident[:]
                )

        with ExitStack() as ph1:
            jpool = ph1.enter_context(tc.tile_pool(name="jpool", bufs=2))
            pss = ph1.enter_context(tc.psum_pool(name="pss", bufs=1))
            pst = ph1.enter_context(tc.psum_pool(name="pst", bufs=6))
            sx_ps = pss.tile([P, (NU // SUMQ) * SP], F32, name="sx_ps")

            m0_ps = pss.tile([P, SP], F32, tag="setup")
            for t in range(SP):
                nc.tensor.matmul(
                    out=m0_ps[:, t : t + 1],
                    lhsT=Y[:, 0, t * P : (t + 1) * P],
                    rhs=ones[:, 0:1],
                    start=True,
                    stop=True,
                )
            nc.scalar.activation(out=negm0[:], in_=m0_ps[:], func=ACT.Copy, scale=-1.0 / P)

            for q in range(NU):
                for t in range(T):
                    tp = pst.tile([P, UC], BF16, tag="tp")
                    transposes(tp, q * UNIT, UNIT, t)
                    if t < SP:
                        junk = jpool.tile([P, UC], BF16, tag="junk")
                        nc.scalar.activation(
                            out=junk[:],
                            in_=tp[:],
                            func=ACT.Square,
                            bias=negm0[:, t : t + 1],
                            accum_out=sq[:, t * NU + q : t * NU + q + 1],
                        )
                    else:
                        nc.vector.bn_stats(out=st[:, t - SP, q, :], in_=tp[:])
                if q % SUMQ == SUMQ - 1:
                    blk = q // SUMQ
                    ng = SUMQ * UNIT
                    for t in range(SP):
                        col = blk * SP + t
                        for j in range(ng):
                            nc.tensor.matmul(
                                out=sx_ps[:, col : col + 1],
                                lhsT=Y[:, blk * ng + j, t * P : (t + 1) * P],
                                rhs=ones[:, 0:1],
                                start=(j == 0),
                                stop=(j == ng - 1),
                            )
                if q == 2:
                    wt_ps = pss.tile([P, T, O], BF16, tag="setup")
                    for t in range(T):
                        for h in range(2):
                            nc.tensor.transpose(
                                wt_ps[:, t, h * P : (h + 1) * P],
                                w_sb[:, h, t * P : (t + 1) * P],
                                ident[:],
                            )
                    nc.scalar.copy(out=wt_sb[:], in_=wt_ps[:])
                    nc.gpsimd.tensor_copy(out=wg[:], in_=wt_sb[:].rearrange("p t o -> p o t"))
                if q == 6:
                    gb_ps = pss.tile([P, P], BF16, tag="setup")
                    nc.tensor.transpose(gb_ps[:], gb[:], ident[:])
                    nc.scalar.copy(out=gbT[:], in_=gb_ps[:, 0 : 2 * T])
                    b2_ps = pss.tile([P, O], F32, tag="setup")
                    nc.tensor.matmul(out=b2_ps[:], lhsT=ones[:], rhs=b2z[:], start=True, stop=True)
                    for h in range(2):
                        nc.scalar.copy(out=b2b[:, h, :], in_=b2_ps[:])

            nc.vector.tensor_reduce(
                out=sxs[:], in_=sx_ps[:].rearrange("p (k t) -> p t k", t=SP), axis=AX.X, op=ALU.add
            )
            nc.vector.bn_aggr(out=mv[:, SP, :], in_=st[:, 0].rearrange("p q s -> p (q s)"))
            nc.vector.scalar_tensor_tensor(
                out=dm[:], in0=sxs[:], scalar=1.0 / B, in1=negm0[:], op0=ALU.mult, op1=ALU.add
            )
            nc.vector.bn_aggr(out=mv[:, SP + 1, :], in_=st[:, 1].rearrange("p q s -> p (q s)"))
            nc.vector.tensor_tensor(out=dm2[:], in0=dm[:], in1=dm[:], op=ALU.mult)
            nc.vector.tensor_reduce(
                out=sqs[:], in_=sq[:].rearrange("p (t q) -> p t q", q=NU), axis=AX.X, op=ALU.add
            )
            nc.vector.tensor_tensor(out=mv[:, 0:SP, 0], in0=dm[:], in1=negm0[:], op=ALU.subtract)
            nc.vector.scalar_tensor_tensor(
                out=mv[:, 0:SP, 1], in0=sqs[:], scalar=1.0 / B, in1=dm2[:], op0=ALU.mult, op1=ALU.subtract
            )
            nc.scalar.activation(out=std[:], in_=mv[:, :, 1], func=ACT.Sqrt, bias=eps[:, 0:1])
            nc.vector.scalar_tensor_tensor(
                out=nmg[:], in0=mv[:, :, 0], scalar=-1.0, in1=gbT[:, 0:T], op0=ALU.mult, op1=ALU.mult
            )
            nc.vector.quantize_mx(
                out=w_codes[:].bitcast(FP8X4),
                scales=w_scales[:],
                in_=wg[:].rearrange("p o t -> p (o t)"),
            )
            nc.vector.reciprocal(out=rstd[:], in_=std[:])

        zpool = ctx.enter_context(tc.tile_pool(name="zpool", bufs=2))
        gpool = ctx.enter_context(tc.tile_pool(name="gpool", bufs=3))
        qpool = ctx.enter_context(tc.tile_pool(name="qpool", bufs=3))
        ppool = ctx.enter_context(tc.tile_pool(name="ppool", bufs=5))
        spool = ctx.enter_context(tc.tile_pool(name="spool", bufs=5))
        kpool = ctx.enter_context(tc.tile_pool(name="kpool", bufs=2))
        ptq = ctx.enter_context(tc.psum_pool(name="ptq", bufs=T))
        psm = ctx.enter_context(tc.psum_pool(name="psm", bufs=CMAX // 2))
        NCH = len(CHUNKS)
        starts = [sum(CHUNKS[:c]) for c in range(NCH)]
        planes, shifted, grouped, codes, scales, sums, rows, norms, inverse = {}, {}, {}, {}, {}, {}, {}, {}, {}

        def transpose_chunk(c):
            planes[c] = []
            for t in range(T):
                tq = ptq.tile([P, CMAX * P], BF16, tag="tq", name="tq")
                transposes(tq, starts[c], CHUNKS[c], t)
                planes[c].append(tq)

        def affine(c):
            width = CHUNKS[c] * P
            shifted[c] = zpool.tile([P, T, CMAX * P], BF16, tag="Z", name="Z")
            for t in range(T):
                nc.vector.tensor_scalar(
                    out=shifted[c][:, t, 0:width],
                    in0=planes[c][t][:, 0:width],
                    scalar1=sc[:, t : t + 1],
                    scalar2=sh[:, t : t + 1],
                    op0=ALU.mult,
                    op1=ALU.add,
                )

        def regroup(c):
            width = CHUNKS[c] * P
            split = width // 4
            grouped[c] = gpool.tile([P, CMAX * P, T], BF16, tag="Gt", name="Gt", align_bytes=64)
            nc.vector.tensor_scalar(
                out=grouped[c][:, 0:split, :].rearrange("p (c i) t -> p c t i", i=4),
                in0=shifted[c][:, :, 0:split].rearrange("p t (c i) -> p c t i", i=4),
                scalar1=0.0,
                scalar2=None,
                op0=ALU.max,
            )
            nc.scalar.activation(
                out=grouped[c][:, split:width, :].rearrange("p (c i) t -> p c t i", i=4),
                in_=shifted[c][:, :, split:width].rearrange("p t (c i) -> p c t i", i=4),
                func=ACT.Relu,
            )

        def quantise_multiply(c):
            width = CHUNKS[c] * P
            codes[c] = qpool.tile([P, CMAX * P], U32, tag="codes", name="codes", align_bytes=64)
            scales[c] = qpool.tile([P, CMAX * P], U8, tag="scales", name="scales", align_bytes=64)
            nc.vector.quantize_mx(
                out=codes[c][:, 0:width].bitcast(FP8X4),
                scales=scales[c][:, 0:width],
                in_=grouped[c][:, 0:width, :].rearrange("p b t -> p (b t)"),
            )
            sums[c] = []
            for i in range(CHUNKS[c] // 2):
                acc = psm.tile([P, 2, O], F32, tag="acc", name="acc")
                sums[c].append(acc)
                for h in range(2):
                    m = slice((2 * i + h) * P, (2 * i + h + 1) * P)
                    nc.tensor.matmul_mx(
                        out=acc[:, h, :],
                        lhsT=codes[c][:, m].bitcast(FP8X4),
                        lhsT_scale=scales[c][:, m],
                        rhs=w_codes[:].bitcast(FP8X4),
                        rhs_scale=w_scales[:],
                        start=True,
                        stop=True,
                    )

        def bias_squares(c):
            tiles = CHUNKS[c]
            rows[c] = ppool.tile([P, CMAX, O], F32, tag="Pt", name="Pt")
            ss = spool.tile([P, CMAX], F32, tag="ss")
            norms[c] = spool.tile([P, CMAX], F32, tag="nrm", name="nrm")
            for i in range(tiles // 2):
                nc.vector.tensor_tensor(
                    out=rows[c][:, 2 * i : 2 * i + 2, :], in0=sums[c][i][:], in1=b2b[:], op=ALU.add
                )
            for r in range(tiles):
                junk2 = kpool.tile([P, O], BF16, tag="junk2")
                nc.scalar.activation(
                    out=junk2[:], in_=rows[c][:, r, :], func=ACT.Square, accum_out=ss[:, r : r + 1]
                )
            nc.scalar.activation(out=norms[c][:, 0:tiles], in_=ss[:, 0:tiles], func=ACT.Sqrt, bias=tiny[:, 0:1])

        def clamp_norm(c):
            tiles = CHUNKS[c]
            nrc = spool.tile([P, CMAX], F32, tag="nrc", name="nrc")
            nc.vector.tensor_scalar(
                out=nrc[:, 0:tiles], in0=norms[c][:, 0:tiles], scalar1=L2_EPS, scalar2=None, op0=ALU.max
            )
            norms[c] = nrc

        def invert_norm(c):
            tiles = CHUNKS[c]
            inverse[c] = spool.tile([P, CMAX], F32, tag="rinv", name="rinv")
            nc.vector.reciprocal(out=inverse[c][:, 0:tiles], in_=norms[c][:, 0:tiles])

        def scale_store(c):
            tiles = CHUNKS[c]
            vector_only = c >= NCH - 2
            for r in range(tiles):
                if r < tiles // 2 and not vector_only:
                    nc.gpsimd.tensor_scalar(
                        out=rows[c][:, r, :],
                        in0=rows[c][:, r, :],
                        scalar1=inverse[c][:, r : r + 1],
                        scalar2=1.0,
                        op0=ALU.mult,
                        op1=ALU.mult,
                    )
                else:
                    nc.vector.tensor_scalar(
                        out=rows[c][:, r, :],
                        in0=rows[c][:, r, :],
                        scalar1=inverse[c][:, r : r + 1],
                        scalar2=None,
                        op0=ALU.mult,
                    )
            nc.sync.dma_start(out=ov[:, starts[c] : starts[c] + tiles, :], in_=rows[c][:, 0:tiles, :])

        transpose_chunk(0)
        nc.vector.tensor_tensor(out=sc[:], in0=gbT[:, 0:T], in1=rstd[:], op=ALU.mult)
        for t in range(T):
            nc.vector.tensor_scalar(
                out=sh[:, t : t + 1],
                in0=rstd[:, t : t + 1],
                scalar1=nmg[:, t : t + 1],
                scalar2=gbT[:, T + t : T + t + 1],
                op0=ALU.mult,
                op1=ALU.add,
            )
        affine(0)
        transpose_chunk(1)
        for i in range(NCH + 2):
            if i < NCH:
                regroup(i)
            if 0 <= i - 2:
                clamp_norm(i - 2)
            if i + 1 < NCH:
                affine(i + 1)
            if i + 2 < NCH:
                transpose_chunk(i + 2)
            if 0 <= i - 2:
                invert_norm(i - 2)
            if 0 <= i - 1 < NCH:
                bias_squares(i - 1)
            if 0 <= i - 2:
                scale_store(i - 2)
            if i < NCH:
                quantise_multiply(i)
